import numpy as np
import ml_dtypes


def mxq(x, axis, fmt="e4m3"):
    dtype, down = {"e4m3": (ml_dtypes.float8_e4m3fn, 7), "e5m2": (ml_dtypes.float8_e5m2, 14)}[fmt]
    v = np.moveaxis(np.asarray(x, np.float32).astype(ml_dtypes.bfloat16).astype(np.float64), axis, -1)
    blocks = v.reshape(v.shape[:-1] + (-1, 32))
    amax = np.abs(blocks).max(-1, keepdims=True)
    byte = np.maximum(np.where(amax > 0, np.frexp(amax)[1] - 1 + 127, 0) - down, 1)
    scale = np.exp2(byte - 127.0)
    codes = (blocks / scale).astype(np.float32).astype(dtype).astype(np.float64)
    return np.moveaxis((codes * scale).reshape(v.shape), -1, axis)


WIDE = False


def mx_kscale(k):
    if not WIDE:
        return np.ones(k)
    levels = np.array([10, -10, 5, -5, 0])
    a = np.random.permutation(np.resize(levels, k // 512 * 4)).reshape(k // 512, 4)
    idx = np.arange(k)
    return np.exp2(a[idx // 512, idx % 128 // 32])


BF16 = ml_dtypes.bfloat16


def bf(x):
    return np.asarray(x, np.float32).astype(BF16)


def f64(x):
    return np.asarray(x).astype(np.float64)


E2M1 = np.array([0.0, 0.5, 1.0, 1.5, 2.0, 3.0, 4.0, 6.0, -0.0, -0.5, -1.0, -1.5, -2.0, -3.0, -4.0, -6.0])


def pack_weight(w, fmt):
    k, n = w.shape
    w = f64(bf(w)).reshape(k // 32, 32, n)
    amax = np.abs(w).max(1)
    if fmt == "e4m3":
        byte = np.frexp(amax)[1] - 1 + 127 - 7
    else:
        mant, ex = np.frexp(amax / 6.0)
        byte = np.where(mant > 0.5, ex, ex - 1) + 127
    byte = np.clip(np.where(amax > 0, byte, 1), 1, 254)
    scaled = (w * np.exp2(127.0 - byte)[:, None, :]).reshape(k, n).astype(np.float32)
    by_word = np.ascontiguousarray(scaled.reshape(k // 512, 128, 4, n).transpose(0, 1, 3, 2))
    if fmt == "e4m3":
        words = by_word.astype(ml_dtypes.float8_e4m3fn).view(np.uint8)
    else:
        c = by_word.astype(ml_dtypes.float4_e2m1fn).view(np.uint8) & 0xF
        words = c[..., 0::2] | (c[..., 1::2] << 4)
    return np.ascontiguousarray(words), np.ascontiguousarray(byte.astype(np.uint8).reshape(k // 512, 16, n))


def unpack_weight(words, scales, fmt):
    g, p, n, _ = words.shape
    if fmt == "e4m3":
        vals = np.ascontiguousarray(words).view(ml_dtypes.float8_e4m3fn).astype(np.float64)
    else:
        nib = np.empty((g, p, n, 4), np.uint8)
        nib[..., 0::2] = words & 0xF
        nib[..., 1::2] = words >> 4
        vals = E2M1[nib]
    vals = vals * np.repeat(np.exp2(scales.astype(np.float64) - 127.0), 8, axis=1)[..., None]
    return vals.transpose(0, 1, 3, 2).reshape(g * 512, n)

def pack4(w):
    words, scales = pack_weight(w, "e2m1")
    return words.reshape(words.shape[0], 128, -1), scales


def unpack4(words, scales):
    return unpack_weight(words.reshape(words.shape[0], 128, -1, 2), scales, "e2m1")


B, S, C, H, D = 2, 128, 1024, 8, 128
E = H * D


def rope_tables():
    inv_freq = 1.0 / (10000.0 ** (np.arange(0, D, 2) / D))
    emb = np.repeat(np.outer(np.arange(S), inv_freq), 2, axis=1)
    return np.cos(emb), np.sin(emb)


def rope(t, cos, sin):
    tr = t[..., 0::2]
    ti = t[..., 1::2]
    t_rot = np.stack([-ti, tr], axis=-1).reshape(t.shape)
    return t * cos + t_rot * sin


def setup_inputs():
    s = mx_kscale(C)
    cos, sin = rope_tables()
    x = bf(np.random.standard_normal((B, S, C)) * s)
    Wq = np.random.standard_normal((E, C)) / np.sqrt(C) / s[None, :]
    Wq_words, Wq_scales = pack4(np.ascontiguousarray(Wq.T))
    bq = bf(np.random.standard_normal(E) * 0.1)
    return {"x": x,
            "cos": bf(cos), "sin": bf(sin),
            "Wq_words": Wq_words, "Wq_scales": Wq_scales,
            "bq": bq}


def reference(x, cos, sin, Wq_words, Wq_scales, bq):
    y = (mxq(f64(x), 2, "e4m3") @ unpack4(Wq_words, Wq_scales)) + f64(bq)
    q = y.reshape(B, S, H, D).transpose(0, 2, 1, 3)
    return np.maximum(rope(q, f64(cos), f64(sin)), 0.0)

@@ -1,0 +1,158 @@
+from contextlib import ExitStack
+
+import concourse.mybir as mybir
+from concourse.masks import make_identity
+
+F32 = mybir.dt.float32
+BF16 = mybir.dt.bfloat16
+I32 = mybir.dt.int32
+U8 = mybir.dt.uint8
+U32 = mybir.dt.uint32
+FP8X4 = mybir.dt.float8_e4m3fn_x4
+FP4X4 = mybir.dt.float4_e2m1fn_x4
+ALU = mybir.AluOpType
+ACT = mybir.ActivationFunctionType
+
+P = 128
+B = 2
+H = 8
+C = 1024
+E = 1024
+K_PASS = 512
+G = C // K_PASS
+HEADS_PER_BANK = 4
+
+FLOPS = 2 * B * P * C * E
+
+
+def tile_lineartransformerblock_pa_s_kernel(tc, x, cos, sin, Wq_words, Wq_scales, bq, out):
+    nc = tc.nc
+    with ExitStack() as ctx:
+        keep = ctx.enter_context(tc.tile_pool(name="keep", bufs=1))
+        psum = ctx.enter_context(tc.psum_pool(name="psum", bufs=1))
+
+        x_sb = keep.tile([P, B, C], BF16)
+        for b in range(B):
+            nc.sync.dma_start(out=x_sb[:, b, :], in_=x[b])
+
+        w_scales = keep.tile([P, G, E], U8, align_bytes=64)
+        nc.vector.memset(w_scales[:].rearrange("p g n -> p (g n)").bitcast(I32), 0)
+        scale_rows = Wq_scales.rearrange("g (q r) n -> r q g n", r=4)
+        for r in range(4):
+            nc.sync.dma_start(out=w_scales[r:P:32, :, :].bitcast(I32), in_=scale_rows[r].bitcast(I32))
+
+        w_bytes = keep.tile([P, G, 2 * E], U8, align_bytes=64)
+        words_by_partition = Wq_words.rearrange("g p n -> p g n")
+        for half in range(2):
+            cols = slice(half * E, (half + 1) * E)
+            nc.sync.dma_start(
+                out=w_bytes[:, :, cols].bitcast(I32), in_=words_by_partition[:, :, cols].bitcast(I32)
+            )
+
+        sin_sb = keep.tile([P, P], BF16)
+        nc.scalar.dma_start(out=sin_sb[:], in_=sin)
+        cos_sb = keep.tile([P, P], BF16)
+        nc.scalar.dma_start(out=cos_sb[:], in_=cos)
+        bias_rows = keep.tile([P, P], BF16)
+        nc.vector.memset(bias_rows[:], 0.0)
+        nc.scalar.dma_start(out=bias_rows[0:H, :], in_=bq.rearrange("(h d) -> h d", d=P))
+
+        ident = keep.tile([P, P], F32)
+        make_identity(nc, ident[:])
+        ident_bf = keep.tile([P, P], BF16)
+        nc.scalar.copy(out=ident_bf[:], in_=ident[:])
+        swap = keep.tile([P, P], F32)
+        ident_pairs = ident[:].rearrange("p (i two) -> p i two", two=2)
+        swap_pairs = swap[:].rearrange("p (i two) -> p i two", two=2)
+        nc.vector.tensor_copy(out=swap_pairs[:, :, 0], in_=ident_pairs[:, :, 1])
+        nc.vector.tensor_copy(out=swap_pairs[:, :, 1], in_=ident_pairs[:, :, 0])
+
+        partner = keep.tile([P, P], BF16)
+        sin_pairs = sin_sb[:].rearrange("p (i two) -> p i two", two=2)
+        partner_pairs = partner[:].rearrange("p (i two) -> p i two", two=2)
+        nc.vector.tensor_copy(out=partner_pairs[:, :, 0], in_=sin_pairs[:, :, 1])
+        nc.vector.tensor_scalar_mul(out=partner_pairs[:, :, 1], in0=sin_pairs[:, :, 0], scalar1=-1.0)
+
+        x_words = x_sb[:].bitcast(F32)
+        grouped = keep.tile([P, B, G * P * 4], BF16, align_bytes=64)
+        x_codes = keep.tile([P, B, G, P], U32, align_bytes=64)
+        x_scales = keep.tile([P, B, G, P], U8, align_bytes=64)
+        for b in range(B):
+            for g in range(G):
+                xt = psum.tile([P, 2, P], F32, tag="bank%d" % (G * b + g))
+                for u in range(2):
+                    nc.tensor.transpose(
+                        xt[:, u, :], x_words[:, b, 256 * g + u : 256 * (g + 1) : 2], ident[:]
+                    )
+                words_out = grouped[:, b, 512 * g : 512 * (g + 1)].bitcast(F32)
+                words_out = words_out.rearrange("p (r u) -> p r u", u=2)
+                if g == 0:
+                    nc.vector.tensor_copy(out=words_out, in_=xt[:].rearrange("p u r -> p r u"))
+                else:
+                    nc.scalar.copy(out=words_out, in_=xt[:].rearrange("p u r -> p r u"))
+            nc.vector.quantize_mx(
+                out=x_codes[:, b].rearrange("p g r -> p (g r)").bitcast(FP8X4),
+                scales=x_scales[:, b].rearrange("p g r -> p (g r)"),
+                in_=grouped[:, b, :],
+            )
+
+        tables_ps = psum.tile([P, 3, P], BF16, tag="bank4")
+        nc.tensor.transpose(tables_ps[:, 0, :], cos_sb[:], ident_bf[:])
+        nc.tensor.transpose(tables_ps[:, 1, :], partner[:], ident_bf[:])
+        nc.tensor.transpose(tables_ps[:, 2, :], bias_rows[:], ident_bf[:])
+        tables = keep.tile([P, 2, P], BF16)
+        nc.scalar.copy(out=tables[:], in_=tables_ps[:, 0:2, :])
+        bias = keep.tile([P, H], F32)
+        nc.scalar.copy(out=bias[:], in_=tables_ps[:, 2, 0:H])
+        cos_both = tables[:, 0, :].unsqueeze(1).to_broadcast([P, B, P])
+        partner_both = tables[:, 1, :].unsqueeze(1).to_broadcast([P, B, P])
+
+        y_banks = []
+        for h in range(H):
+            yT = psum.tile([P, B, P], F32, tag="bank%d" % h)
+            y_banks.append(yT)
+            for b in range(B):
+                for g in range(G):
+                    nc.tensor.matmul_mx(
+                        out=yT[:, b, :],
+                        lhsT=w_bytes[:, g, 2 * P * h : 2 * P * (h + 1)].bitcast(FP4X4),
+                        lhsT_scale=w_scales[:, g, P * h : P * (h + 1)],
+                        rhs=x_codes[:, b, g, :].bitcast(FP8X4),
+                        rhs_scale=x_scales[:, b, g, :],
+                        start=(g == 0),
+                        stop=(g == G - 1),
+                    )
+
+        own = keep.tile([P, H, B, P], F32)
+        cross = keep.tile([P, H, B, P], F32)
+        result = keep.tile([P, B, H, P], F32)
+        for group in range(H // HEADS_PER_BANK):
+            heads = range(group * HEADS_PER_BANK, (group + 1) * HEADS_PER_BANK)
+            for h in heads:
+                nc.vector.scalar_tensor_tensor(
+                    out=own[:, h], in0=y_banks[h][:], scalar=bias[:, h : h + 1], in1=cos_both,
+                    op0=ALU.add, op1=ALU.mult,
+                )
+                nc.vector.scalar_tensor_tensor(
+                    out=cross[:, h], in0=y_banks[h][:], scalar=bias[:, h : h + 1], in1=partner_both,
+                    op0=ALU.add, op1=ALU.mult,
+                )
+            rope_banks = []
+            for b in range(B):
+                rope_ps = psum.tile([P, HEADS_PER_BANK, P], F32, tag="bank%d" % (B * group + b))
+                rope_banks.append(rope_ps)
+            for h in heads:
+                for b in range(B):
+                    spot = rope_banks[b][:, h % HEADS_PER_BANK, :]
+                    nc.tensor.matmul(
+                        out=spot, lhsT=own[:, h, b, :], rhs=ident[:], is_transpose=True, start=True, stop=False
+                    )
+                    nc.tensor.matmul(
+                        out=spot, lhsT=cross[:, h, b, :], rhs=swap[:], is_transpose=True, start=False, stop=True
+                    )
+            for b in range(B):
+                head_cols = slice(group * HEADS_PER_BANK, (group + 1) * HEADS_PER_BANK)
+                nc.scalar.activation(out=result[:, b, head_cols, :], in_=rope_banks[b][:], func=ACT.Relu)
+                nc.sync.dma_start(
+                    out=out[b, head_cols].rearrange("h s d -> s h d"), in_=result[:, b, head_cols, :]
+                )

@@ -20,7 +20,7 @@ C = 1024
 E = 1024
 K_PASS = 512
 G = C // K_PASS
-HEADS_PER_BANK = 4
+PAIRS = H // 2
 
 FLOPS = 2 * B * P * C * E
 
@@ -96,7 +96,7 @@ def tile_lineartransformerblock_pa_s_kernel(tc, x, cos, sin, Wq_words, Wq_scales
                 in_=grouped[:, b, :],
             )
 
-        tables_ps = psum.tile([P, 3, P], BF16, tag="bank4")
+        tables_ps = psum.tile([P, 3, P], BF16, tag="bank7")
         nc.tensor.transpose(tables_ps[:, 0, :], cos_sb[:], ident_bf[:])
         nc.tensor.transpose(tables_ps[:, 1, :], partner[:], ident_bf[:])
         nc.tensor.transpose(tables_ps[:, 2, :], bias_rows[:], ident_bf[:])
@@ -104,55 +104,52 @@ def tile_lineartransformerblock_pa_s_kernel(tc, x, cos, sin, Wq_words, Wq_scales
         nc.scalar.copy(out=tables[:], in_=tables_ps[:, 0:2, :])
         bias = keep.tile([P, H], F32)
         nc.scalar.copy(out=bias[:], in_=tables_ps[:, 2, 0:H])
-        cos_both = tables[:, 0, :].unsqueeze(1).to_broadcast([P, B, P])
-        partner_both = tables[:, 1, :].unsqueeze(1).to_broadcast([P, B, P])
 
-        y_banks = []
-        for h in range(H):
-            yT = psum.tile([P, B, P], F32, tag="bank%d" % h)
-            y_banks.append(yT)
-            for b in range(B):
-                for g in range(G):
-                    nc.tensor.matmul_mx(
-                        out=yT[:, b, :],
-                        lhsT=w_bytes[:, g, 2 * P * h : 2 * P * (h + 1)].bitcast(FP4X4),
-                        lhsT_scale=w_scales[:, g, P * h : P * (h + 1)],
-                        rhs=x_codes[:, b, g, :].bitcast(FP8X4),
-                        rhs_scale=x_scales[:, b, g, :],
-                        start=(g == 0),
-                        stop=(g == G - 1),
-                    )
+        y_banks = {}
+        for b in range(B):
+            for pair in range(PAIRS):
+                yT = psum.tile([P, 2, P], F32, tag="bank%d" % ((PAIRS * (b + 1) + pair) % 8))
+                y_banks[(b, pair)] = yT
+                for i in range(2):
+                    h = 2 * pair + i
+                    for g in range(G):
+                        nc.tensor.matmul_mx(
+                            out=yT[:, i, :],
+                            lhsT=w_bytes[:, g, 2 * P * h : 2 * P * (h + 1)].bitcast(FP4X4),
+                            lhsT_scale=w_scales[:, g, P * h : P * (h + 1)],
+                            rhs=x_codes[:, b, g, :].bitcast(FP8X4),
+                            rhs_scale=x_scales[:, b, g, :],
+                            start=(g == 0),
+                            stop=(g == G - 1),
+                        )
 
-        own = keep.tile([P, H, B, P], F32)
-        cross = keep.tile([P, H, B, P], F32)
+        own = keep.tile([P, B, H, P], F32)
+        cross = keep.tile([P, B, H, P], F32)
         result = keep.tile([P, B, H, P], F32)
-        for group in range(H // HEADS_PER_BANK):
-            heads = range(group * HEADS_PER_BANK, (group + 1) * HEADS_PER_BANK)
-            for h in heads:
-                nc.vector.scalar_tensor_tensor(
-                    out=own[:, h], in0=y_banks[h][:], scalar=bias[:, h : h + 1], in1=cos_both,
-                    op0=ALU.add, op1=ALU.mult,
-                )
-                nc.vector.scalar_tensor_tensor(
-                    out=cross[:, h], in0=y_banks[h][:], scalar=bias[:, h : h + 1], in1=partner_both,
-                    op0=ALU.add, op1=ALU.mult,
-                )
-            rope_banks = []
-            for b in range(B):
-                rope_ps = psum.tile([P, HEADS_PER_BANK, P], F32, tag="bank%d" % (B * group + b))
-                rope_banks.append(rope_ps)
-            for h in heads:
-                for b in range(B):
-                    spot = rope_banks[b][:, h % HEADS_PER_BANK, :]
+        for b in range(B):
+            for pair in range(PAIRS):
+                yT = y_banks[(b, pair)]
+                for i in range(2):
+                    h = 2 * pair + i
+                    nc.vector.scalar_tensor_tensor(
+                        out=own[:, b, h, :], in0=yT[:, i, :], scalar=bias[:, h : h + 1], in1=tables[:, 0, :],
+                        op0=ALU.add, op1=ALU.mult,
+                    )
+                    nc.vector.scalar_tensor_tensor(
+                        out=cross[:, b, h, :], in0=yT[:, i, :], scalar=bias[:, h : h + 1], in1=tables[:, 1, :],
+                        op0=ALU.add, op1=ALU.mult,
+                    )
+                rope_ps = psum.tile([P, 2, P], F32, tag="bank%d" % ((PAIRS * (b + 1) + pair) % 8))
+                for i in range(2):
+                    h = 2 * pair + i
                     nc.tensor.matmul(
-                        out=spot, lhsT=own[:, h, b, :], rhs=ident[:], is_transpose=True, start=True, stop=False
+                        out=rope_ps[:, i, :], lhsT=own[:, b, h, :], rhs=ident[:],
+                        is_transpose=True, start=True, stop=False,
                     )
                     nc.tensor.matmul(
-                        out=spot, lhsT=cross[:, h, b, :], rhs=swap[:], is_transpose=True, start=False, stop=True
+                        out=rope_ps[:, i, :], lhsT=cross[:, b, h, :], rhs=swap[:],
+                        is_transpose=True, start=False, stop=True,
                     )
-            for b in range(B):
-                head_cols = slice(group * HEADS_PER_BANK, (group + 1) * HEADS_PER_BANK)
-                nc.scalar.activation(out=result[:, b, head_cols, :], in_=rope_banks[b][:], func=ACT.Relu)
-                nc.sync.dma_start(
-                    out=out[b, head_cols].rearrange("h s d -> s h d"), in_=result[:, b, head_cols, :]
-                )
+                heads = slice(2 * pair, 2 * pair + 2)
+                nc.scalar.activation(out=result[:, b, heads, :], in_=rope_ps[:], func=ACT.Relu)
+                nc.sync.dma_start(out=out[b, heads].rearrange("h s d -> s h d"), in_=result[:, b, heads, :])

@@ -86,15 +86,12 @@ def tile_lineartransformerblock_pa_s_kernel(tc, x, cos, sin, Wq_words, Wq_scales
                     )
                 words_out = grouped[:, b, 512 * g : 512 * (g + 1)].bitcast(F32)
                 words_out = words_out.rearrange("p (r u) -> p r u", u=2)
-                if g == 0:
-                    nc.vector.tensor_copy(out=words_out, in_=xt[:].rearrange("p u r -> p r u"))
-                else:
-                    nc.scalar.copy(out=words_out, in_=xt[:].rearrange("p u r -> p r u"))
-            nc.vector.quantize_mx(
-                out=x_codes[:, b].rearrange("p g r -> p (g r)").bitcast(FP8X4),
-                scales=x_scales[:, b].rearrange("p g r -> p (g r)"),
-                in_=grouped[:, b, :],
-            )
+                nc.scalar.copy(out=words_out, in_=xt[:].rearrange("p u r -> p r u"))
+                nc.vector.quantize_mx(
+                    out=x_codes[:, b, g, :].bitcast(FP8X4),
+                    scales=x_scales[:, b, g, :],
+                    in_=grouped[:, b, 512 * g : 512 * (g + 1)],
+                )
 
         tables_ps = psum.tile([P, 3, P], BF16, tag="bank7")
         nc.tensor.transpose(tables_ps[:, 0, :], cos_sb[:], ident_bf[:])
@@ -123,8 +120,7 @@ def tile_lineartransformerblock_pa_s_kernel(tc, x, cos, sin, Wq_words, Wq_scales
                             stop=(g == G - 1),
                         )
 
-        own = keep.tile([P, B, H, P], F32)
-        cross = keep.tile([P, B, H, P], F32)
+        products = keep.tile([P, B, H, 2, P], F32)
         result = keep.tile([P, B, H, P], F32)
         for b in range(B):
             for pair in range(PAIRS):
@@ -132,22 +128,19 @@ def tile_lineartransformerblock_pa_s_kernel(tc, x, cos, sin, Wq_words, Wq_scales
                 for i in range(2):
                     h = 2 * pair + i
                     nc.vector.scalar_tensor_tensor(
-                        out=own[:, b, h, :], in0=yT[:, i, :], scalar=bias[:, h : h + 1], in1=tables[:, 0, :],
-                        op0=ALU.add, op1=ALU.mult,
-                    )
-                    nc.vector.scalar_tensor_tensor(
-                        out=cross[:, b, h, :], in0=yT[:, i, :], scalar=bias[:, h : h + 1], in1=tables[:, 1, :],
+                        out=products[:, b, h, :, :], in0=yT[:, i : i + 1, :].to_broadcast([P, 2, P]),
+                        scalar=bias[:, h : h + 1], in1=tables[:],
                         op0=ALU.add, op1=ALU.mult,
                     )
                 rope_ps = psum.tile([P, 2, P], F32, tag="bank%d" % ((PAIRS * (b + 1) + pair) % 8))
                 for i in range(2):
                     h = 2 * pair + i
                     nc.tensor.matmul(
-                        out=rope_ps[:, i, :], lhsT=own[:, b, h, :], rhs=ident[:],
+                        out=rope_ps[:, i, :], lhsT=products[:, b, h, 0, :], rhs=ident[:],
                         is_transpose=True, start=True, stop=False,
                     )
                     nc.tensor.matmul(
-                        out=rope_ps[:, i, :], lhsT=cross[:, b, h, :], rhs=swap[:],
+                        out=rope_ps[:, i, :], lhsT=products[:, b, h, 1, :], rhs=swap[:],
                         is_transpose=True, start=False, stop=True,
                     )
                 heads = slice(2 * pair, 2 * pair + 2)

@@ -21,6 +21,9 @@ E = 1024
 K_PASS = 512
 G = C // K_PASS
 PAIRS = H // 2
+SIDE_ROAD = [(0, 0), (1, 0)]
+CLOSING_ORDER = [(0, 1), (0, 2), (0, 3), (0, 0), (1, 1), (1, 2), (1, 3), (1, 0)]
+TABLES_AFTER = 2
 
 FLOPS = 2 * B * P * C * E
 
@@ -30,6 +33,7 @@ def tile_lineartransformerblock_pa_s_kernel(tc, x, cos, sin, Wq_words, Wq_scales
     with ExitStack() as ctx:
         keep = ctx.enter_context(tc.tile_pool(name="keep", bufs=1))
         psum = ctx.enter_context(tc.psum_pool(name="psum", bufs=1))
+        ctx.enter_context(tc.manual_schedule())
 
         x_sb = keep.tile([P, B, C], BF16)
         for b in range(B):
@@ -50,12 +54,12 @@ def tile_lineartransformerblock_pa_s_kernel(tc, x, cos, sin, Wq_words, Wq_scales
             )
 
         sin_sb = keep.tile([P, P], BF16)
-        nc.scalar.dma_start(out=sin_sb[:], in_=sin)
+        nc.sync.dma_start(out=sin_sb[:], in_=sin)
         cos_sb = keep.tile([P, P], BF16)
-        nc.scalar.dma_start(out=cos_sb[:], in_=cos)
+        nc.sync.dma_start(out=cos_sb[:], in_=cos)
         bias_rows = keep.tile([P, P], BF16)
         nc.vector.memset(bias_rows[:], 0.0)
-        nc.scalar.dma_start(out=bias_rows[0:H, :], in_=bq.rearrange("(h d) -> h d", d=P))
+        nc.sync.dma_start(out=bias_rows[0:H, :], in_=bq.rearrange("(h d) -> h d", d=P))
 
         ident = keep.tile([P, P], F32)
         make_identity(nc, ident[:])
@@ -66,12 +70,6 @@ def tile_lineartransformerblock_pa_s_kernel(tc, x, cos, sin, Wq_words, Wq_scales
         swap_pairs = swap[:].rearrange("p (i two) -> p i two", two=2)
         nc.vector.tensor_copy(out=swap_pairs[:, :, 0], in_=ident_pairs[:, :, 1])
         nc.vector.tensor_copy(out=swap_pairs[:, :, 1], in_=ident_pairs[:, :, 0])
-
-        partner = keep.tile([P, P], BF16)
-        sin_pairs = sin_sb[:].rearrange("p (i two) -> p i two", two=2)
-        partner_pairs = partner[:].rearrange("p (i two) -> p i two", two=2)
-        nc.vector.tensor_copy(out=partner_pairs[:, :, 0], in_=sin_pairs[:, :, 1])
-        nc.vector.tensor_scalar_mul(out=partner_pairs[:, :, 1], in0=sin_pairs[:, :, 0], scalar1=-1.0)
 
         x_words = x_sb[:].bitcast(F32)
         grouped = keep.tile([P, B, G * P * 4], BF16, align_bytes=64)
@@ -93,56 +91,95 @@ def tile_lineartransformerblock_pa_s_kernel(tc, x, cos, sin, Wq_words, Wq_scales
                     in_=grouped[:, b, 512 * g : 512 * (g + 1)],
                 )
 
-        tables_ps = psum.tile([P, 3, P], BF16, tag="bank7")
+        y_banks = {}
+
+        def multiply(b, pair):
+            yT = psum.tile([P, 2, P], F32, tag="bank%d" % ((PAIRS * (b + 1) + pair) % 8))
+            y_banks[(b, pair)] = yT
+            for i in range(2):
+                h = 2 * pair + i
+                for g in range(G):
+                    nc.tensor.matmul_mx(
+                        out=yT[:, i, :],
+                        lhsT=w_bytes[:, g, 2 * P * h : 2 * P * (h + 1)].bitcast(FP4X4),
+                        lhsT_scale=w_scales[:, g, P * h : P * (h + 1)],
+                        rhs=x_codes[:, b, g, :].bitcast(FP8X4),
+                        rhs_scale=x_scales[:, b, g, :],
+                        start=(g == 0),
+                        stop=(g == G - 1),
+                    )
+
+        for pair in range(TABLES_AFTER):
+            multiply(0, pair)
+
+        partner = keep.tile([P, P], BF16)
+        sin_pairs = sin_sb[:].rearrange("p (i two) -> p i two", two=2)
+        partner_pairs = partner[:].rearrange("p (i two) -> p i two", two=2)
+        nc.vector.tensor_copy(out=partner_pairs[:, :, 0], in_=sin_pairs[:, :, 1])
+        nc.vector.tensor_scalar_mul(out=partner_pairs[:, :, 1], in0=sin_pairs[:, :, 0], scalar1=-1.0)
+
+        tables_ps = psum.tile([P, 3, P], BF16, tag="bank3")
         nc.tensor.transpose(tables_ps[:, 0, :], cos_sb[:], ident_bf[:])
         nc.tensor.transpose(tables_ps[:, 1, :], partner[:], ident_bf[:])
         nc.tensor.transpose(tables_ps[:, 2, :], bias_rows[:], ident_bf[:])
         tables = keep.tile([P, 2, P], BF16)
-        nc.scalar.copy(out=tables[:], in_=tables_ps[:, 0:2, :])
+        nc.vector.tensor_copy(out=tables[:], in_=tables_ps[:, 0:2, :])
         bias = keep.tile([P, H], F32)
-        nc.scalar.copy(out=bias[:], in_=tables_ps[:, 2, 0:H])
+        nc.vector.tensor_copy(out=bias[:], in_=tables_ps[:, 2, 0:H])
 
-        y_banks = {}
-        for b in range(B):
-            for pair in range(PAIRS):
-                yT = psum.tile([P, 2, P], F32, tag="bank%d" % ((PAIRS * (b + 1) + pair) % 8))
-                y_banks[(b, pair)] = yT
-                for i in range(2):
-                    h = 2 * pair + i
-                    for g in range(G):
-                        nc.tensor.matmul_mx(
-                            out=yT[:, i, :],
-                            lhsT=w_bytes[:, g, 2 * P * h : 2 * P * (h + 1)].bitcast(FP4X4),
-                            lhsT_scale=w_scales[:, g, P * h : P * (h + 1)],
-                            rhs=x_codes[:, b, g, :].bitcast(FP8X4),
-                            rhs_scale=x_scales[:, b, g, :],
-                            start=(g == 0),
-                            stop=(g == G - 1),
-                        )
+        for pair in range(TABLES_AFTER, PAIRS):
+            multiply(0, pair)
+        for pair in range(PAIRS):
+            multiply(1, pair)
 
         products = keep.tile([P, B, H, 2, P], F32)
         result = keep.tile([P, B, H, P], F32)
-        for b in range(B):
-            for pair in range(PAIRS):
-                yT = y_banks[(b, pair)]
-                for i in range(2):
-                    h = 2 * pair + i
-                    nc.vector.scalar_tensor_tensor(
-                        out=products[:, b, h, :, :], in0=yT[:, i : i + 1, :].to_broadcast([P, 2, P]),
-                        scalar=bias[:, h : h + 1], in1=tables[:],
-                        op0=ALU.add, op1=ALU.mult,
-                    )
-                rope_ps = psum.tile([P, 2, P], F32, tag="bank%d" % ((PAIRS * (b + 1) + pair) % 8))
-                for i in range(2):
-                    h = 2 * pair + i
-                    nc.tensor.matmul(
-                        out=rope_ps[:, i, :], lhsT=products[:, b, h, 0, :], rhs=ident[:],
-                        is_transpose=True, start=True, stop=False,
-                    )
-                    nc.tensor.matmul(
-                        out=rope_ps[:, i, :], lhsT=products[:, b, h, 1, :], rhs=swap[:],
-                        is_transpose=True, start=False, stop=True,
-                    )
-                heads = slice(2 * pair, 2 * pair + 2)
-                nc.scalar.activation(out=result[:, b, heads, :], in_=rope_ps[:], func=ACT.Relu)
-                nc.sync.dma_start(out=out[b, heads].rearrange("h s d -> s h d"), in_=result[:, b, heads, :])
+        shifted = keep.tile([P, len(SIDE_ROAD), 2, P], F32)
+
+        def multiply_by_tables_on_vector(b, pair):
+            yT = y_banks[(b, pair)]
+            for i in range(2):
+                h = 2 * pair + i
+                nc.vector.scalar_tensor_tensor(
+                    out=products[:, b, h, :, :], in0=yT[:, i : i + 1, :].to_broadcast([P, 2, P]),
+                    scalar=bias[:, h : h + 1], in1=tables[:],
+                    op0=ALU.add, op1=ALU.mult,
+                )
+
+        def multiply_by_tables_on_gpsimd(b, pair):
+            yT = y_banks[(b, pair)]
+            slot = SIDE_ROAD.index((b, pair))
+            for i in range(2):
+                h = 2 * pair + i
+                nc.scalar.activation(
+                    out=shifted[:, slot, i, :], in_=yT[:, i, :], func=ACT.Identity, bias=bias[:, h : h + 1], scale=1.0
+                )
+            for i in range(2):
+                h = 2 * pair + i
+                nc.gpsimd.tensor_tensor(
+                    out=products[:, b, h, :, :], in0=shifted[:, slot, i : i + 1, :].to_broadcast([P, 2, P]),
+                    in1=tables[:], op=ALU.mult,
+                )
+
+        def turn_back_and_store(b, pair):
+            rope_ps = psum.tile([P, 2, P], F32, tag="bank%d" % ((PAIRS * (b + 1) + pair) % 8))
+            for i in range(2):
+                h = 2 * pair + i
+                nc.tensor.matmul(
+                    out=rope_ps[:, i, :], lhsT=products[:, b, h, 0, :], rhs=ident[:],
+                    is_transpose=True, start=True, stop=False,
+                )
+                nc.tensor.matmul(
+                    out=rope_ps[:, i, :], lhsT=products[:, b, h, 1, :], rhs=swap[:],
+                    is_transpose=True, start=False, stop=True,
+                )
+            heads = slice(2 * pair, 2 * pair + 2)
+            nc.scalar.activation(out=result[:, b, heads, :], in_=rope_ps[:], func=ACT.Relu)
+            nc.sync.dma_start(out=out[b, heads].rearrange("h s d -> s h d"), in_=result[:, b, heads, :])
+
+        for b, pair in SIDE_ROAD:
+            multiply_by_tables_on_gpsimd(b, pair)
+        for b, pair in CLOSING_ORDER:
+            if (b, pair) not in SIDE_ROAD:
+                multiply_by_tables_on_vector(b, pair)
+            turn_back_and_store(b, pair)

@@ -23,6 +23,7 @@ G = C // K_PASS
 PAIRS = H // 2
 SIDE_ROAD = [(0, 0), (1, 0)]
 CLOSING_ORDER = [(0, 1), (0, 2), (0, 3), (0, 0), (1, 1), (1, 2), (1, 3), (1, 0)]
+WARM_UP = 3
 TABLES_AFTER = 2
 
 FLOPS = 2 * B * P * C * E
@@ -34,6 +35,12 @@ def tile_lineartransformerblock_pa_s_kernel(tc, x, cos, sin, Wq_words, Wq_scales
         keep = ctx.enter_context(tc.tile_pool(name="keep", bufs=1))
         psum = ctx.enter_context(tc.psum_pool(name="psum", bufs=1))
         ctx.enter_context(tc.manual_schedule())
+
+        ones = keep.tile([P, 4 * P], BF16)
+        nc.vector.memset(ones[:], 1.0)
+        for i in range(WARM_UP):
+            idle_ps = psum.tile([P, 4 * P], F32, tag="bank5")
+            nc.tensor.matmul(out=idle_ps[:], lhsT=ones[:, 0:P], rhs=ones[:], start=True, stop=True)
 
         x_sb = keep.tile([P, B, C], BF16)
         for b in range(B):

@@ -24,6 +24,7 @@ PAIRS = H // 2
 SIDE_ROAD = [(0, 0), (1, 0)]
 CLOSING_ORDER = [(0, 1), (0, 2), (0, 3), (0, 0), (1, 1), (1, 2), (1, 3), (1, 0)]
 WARM_UP = 3
+FINE_END = 2
 TABLES_AFTER = 2
 
 FLOPS = 2 * B * P * C * E
@@ -168,25 +169,40 @@ def tile_lineartransformerblock_pa_s_kernel(tc, x, cos, sin, Wq_words, Wq_scales
                     in1=tables[:], op=ALU.mult,
                 )
 
-        def turn_back_and_store(b, pair):
-            rope_ps = psum.tile([P, 2, P], F32, tag="bank%d" % ((PAIRS * (b + 1) + pair) % 8))
-            for i in range(2):
-                h = 2 * pair + i
-                nc.tensor.matmul(
-                    out=rope_ps[:, i, :], lhsT=products[:, b, h, 0, :], rhs=ident[:],
-                    is_transpose=True, start=True, stop=False,
-                )
-                nc.tensor.matmul(
-                    out=rope_ps[:, i, :], lhsT=products[:, b, h, 1, :], rhs=swap[:],
-                    is_transpose=True, start=False, stop=True,
-                )
-            heads = slice(2 * pair, 2 * pair + 2)
-            nc.scalar.activation(out=result[:, b, heads, :], in_=rope_ps[:], func=ACT.Relu)
-            nc.sync.dma_start(out=out[b, heads].rearrange("h s d -> s h d"), in_=result[:, b, heads, :])
+        def turn_back_and_store(b, pair, by_head):
+            if by_head:
+                for i in range(2):
+                    h = 2 * pair + i
+                    head_ps = psum.tile([P, P], F32, tag="bank%d" % (PAIRS + (2 * pair + i) % PAIRS))
+                    nc.tensor.matmul(
+                        out=head_ps[:], lhsT=products[:, b, h, 0, :], rhs=ident[:],
+                        is_transpose=True, start=True, stop=False,
+                    )
+                    nc.tensor.matmul(
+                        out=head_ps[:], lhsT=products[:, b, h, 1, :], rhs=swap[:],
+                        is_transpose=True, start=False, stop=True,
+                    )
+                    nc.scalar.activation(out=result[:, b, h, :], in_=head_ps[:], func=ACT.Relu)
+                    nc.sync.dma_start(out=out[b, h], in_=result[:, b, h, :])
+            else:
+                rope_ps = psum.tile([P, 2, P], F32, tag="bank%d" % ((PAIRS * (b + 1) + pair) % 8))
+                for i in range(2):
+                    h = 2 * pair + i
+                    nc.tensor.matmul(
+                        out=rope_ps[:, i, :], lhsT=products[:, b, h, 0, :], rhs=ident[:],
+                        is_transpose=True, start=True, stop=False,
+                    )
+                    nc.tensor.matmul(
+                        out=rope_ps[:, i, :], lhsT=products[:, b, h, 1, :], rhs=swap[:],
+                        is_transpose=True, start=False, stop=True,
+                    )
+                heads = slice(2 * pair, 2 * pair + 2)
+                nc.scalar.activation(out=result[:, b, heads, :], in_=rope_ps[:], func=ACT.Relu)
+                nc.sync.dma_start(out=out[b, heads].rearrange("h s d -> s h d"), in_=result[:, b, heads, :])
 
         for b, pair in SIDE_ROAD:
             multiply_by_tables_on_gpsimd(b, pair)
         for b, pair in CLOSING_ORDER:
             if (b, pair) not in SIDE_ROAD:
                 multiply_by_tables_on_vector(b, pair)
-            turn_back_and_store(b, pair)
+            turn_back_and_store(b, pair, by_head=(b, pair) in CLOSING_ORDER[-FINE_END:])

@@ -21,8 +21,8 @@ E = 1024
 K_PASS = 512
 G = C // K_PASS
 PAIRS = H // 2
-SIDE_ROAD = [(0, 0), (1, 0)]
-CLOSING_ORDER = [(0, 1), (0, 2), (0, 3), (0, 0), (1, 1), (1, 2), (1, 3), (1, 0)]
+SIDE_HEADS = [(0, 0), (0, 1), (1, 0)]
+CLOSING_ORDER = [(0, 1), (0, 2), (0, 3), (0, 0), (1, 1), (1, 2), (1, 0), (1, 3)]
 WARM_UP = 3
 FINE_END = 2
 TABLES_AFTER = 2
@@ -142,32 +142,26 @@ def tile_lineartransformerblock_pa_s_kernel(tc, x, cos, sin, Wq_words, Wq_scales
 
         products = keep.tile([P, B, H, 2, P], F32)
         result = keep.tile([P, B, H, P], F32)
-        shifted = keep.tile([P, len(SIDE_ROAD), 2, P], F32)
+        shifted = keep.tile([P, len(SIDE_HEADS), P], F32)
 
-        def multiply_by_tables_on_vector(b, pair):
-            yT = y_banks[(b, pair)]
-            for i in range(2):
-                h = 2 * pair + i
-                nc.vector.scalar_tensor_tensor(
-                    out=products[:, b, h, :, :], in0=yT[:, i : i + 1, :].to_broadcast([P, 2, P]),
-                    scalar=bias[:, h : h + 1], in1=tables[:],
-                    op0=ALU.add, op1=ALU.mult,
-                )
+        def multiply_by_tables_on_vector(b, h):
+            yT = y_banks[(b, h // 2)]
+            nc.vector.scalar_tensor_tensor(
+                out=products[:, b, h, :, :], in0=yT[:, h % 2 : h % 2 + 1, :].to_broadcast([P, 2, P]),
+                scalar=bias[:, h : h + 1], in1=tables[:],
+                op0=ALU.add, op1=ALU.mult,
+            )
 
-        def multiply_by_tables_on_gpsimd(b, pair):
-            yT = y_banks[(b, pair)]
-            slot = SIDE_ROAD.index((b, pair))
-            for i in range(2):
-                h = 2 * pair + i
-                nc.scalar.activation(
-                    out=shifted[:, slot, i, :], in_=yT[:, i, :], func=ACT.Identity, bias=bias[:, h : h + 1], scale=1.0
-                )
-            for i in range(2):
-                h = 2 * pair + i
-                nc.gpsimd.tensor_tensor(
-                    out=products[:, b, h, :, :], in0=shifted[:, slot, i : i + 1, :].to_broadcast([P, 2, P]),
-                    in1=tables[:], op=ALU.mult,
-                )
+        def multiply_by_tables_on_gpsimd(b, h):
+            yT = y_banks[(b, h // 2)]
+            slot = SIDE_HEADS.index((b, h))
+            nc.scalar.activation(
+                out=shifted[:, slot, :], in_=yT[:, h % 2, :], func=ACT.Identity, bias=bias[:, h : h + 1], scale=1.0
+            )
+            nc.gpsimd.tensor_tensor(
+                out=products[:, b, h, :, :], in0=shifted[:, slot : slot + 1, :].to_broadcast([P, 2, P]),
+                in1=tables[:], op=ALU.mult,
+            )
 
         def turn_back_and_store(b, pair, by_head):
             if by_head:
@@ -200,9 +194,10 @@ def tile_lineartransformerblock_pa_s_kernel(tc, x, cos, sin, Wq_words, Wq_scales
                 nc.scalar.activation(out=result[:, b, heads, :], in_=rope_ps[:], func=ACT.Relu)
                 nc.sync.dma_start(out=out[b, heads].rearrange("h s d -> s h d"), in_=result[:, b, heads, :])
 
-        for b, pair in SIDE_ROAD:
-            multiply_by_tables_on_gpsimd(b, pair)
+        for b, h in SIDE_HEADS:
+            multiply_by_tables_on_gpsimd(b, h)
         for b, pair in CLOSING_ORDER:
-            if (b, pair) not in SIDE_ROAD:
-                multiply_by_tables_on_vector(b, pair)
+            for h in (2 * pair, 2 * pair + 1):
+                if (b, h) not in SIDE_HEADS:
+                    multiply_by_tables_on_vector(b, h)
             turn_back_and_store(b, pair, by_head=(b, pair) in CLOSING_ORDER[-FINE_END:])

@@ -24,7 +24,7 @@ PAIRS = H // 2
 SIDE_HEADS = [(0, 0), (0, 1), (1, 0)]
 CLOSING_ORDER = [(0, 1), (0, 2), (0, 3), (0, 0), (1, 1), (1, 2), (1, 0), (1, 3)]
 WARM_UP = 3
-FINE_END = 2
+ROW_TOKENS = 2
 TABLES_AFTER = 2
 
 FLOPS = 2 * B * P * C * E
@@ -91,8 +91,8 @@ def tile_lineartransformerblock_pa_s_kernel(tc, x, cos, sin, Wq_words, Wq_scales
                         xt[:, u, :], x_words[:, b, 256 * g + u : 256 * (g + 1) : 2], ident[:]
                     )
                 words_out = grouped[:, b, 512 * g : 512 * (g + 1)].bitcast(F32)
-                words_out = words_out.rearrange("p (r u) -> p r u", u=2)
-                nc.scalar.copy(out=words_out, in_=xt[:].rearrange("p u r -> p r u"))
+                words_out = words_out.rearrange("p (j t u) -> p j t u", j=ROW_TOKENS, u=2)
+                nc.scalar.copy(out=words_out, in_=xt[:].rearrange("p u (t j) -> p j t u", j=ROW_TOKENS))
                 nc.vector.quantize_mx(
                     out=x_codes[:, b, g, :].bitcast(FP8X4),
                     scales=x_scales[:, b, g, :],
@@ -131,7 +131,10 @@ def tile_lineartransformerblock_pa_s_kernel(tc, x, cos, sin, Wq_words, Wq_scales
         nc.tensor.transpose(tables_ps[:, 1, :], partner[:], ident_bf[:])
         nc.tensor.transpose(tables_ps[:, 2, :], bias_rows[:], ident_bf[:])
         tables = keep.tile([P, 2, P], BF16)
-        nc.vector.tensor_copy(out=tables[:], in_=tables_ps[:, 0:2, :])
+        nc.vector.tensor_copy(
+            out=tables[:].rearrange("p w (j t) -> p w j t", j=ROW_TOKENS),
+            in_=tables_ps[:, 0:2, :].rearrange("p w (t j) -> p w j t", j=ROW_TOKENS),
+        )
         bias = keep.tile([P, H], F32)
         nc.vector.tensor_copy(out=bias[:], in_=tables_ps[:, 2, 0:H])
 
@@ -140,15 +143,20 @@ def tile_lineartransformerblock_pa_s_kernel(tc, x, cos, sin, Wq_words, Wq_scales
         for pair in range(PAIRS):
             multiply(1, pair)
 
-        products = keep.tile([P, B, H, 2, P], F32)
-        result = keep.tile([P, B, H, P], F32)
+        TG = P // ROW_TOKENS
+        products = keep.tile([P, B, PAIRS, 2, ROW_TOKENS, 2, TG], F32)
+        result = keep.tile([P, B, PAIRS, ROW_TOKENS, P], F32)
         shifted = keep.tile([P, len(SIDE_HEADS), P], F32)
+        tables_by_row = tables[:].rearrange("p w (j t) -> p w j t", j=ROW_TOKENS)
+
+        def twice(values):
+            return values.rearrange("p o (j t) -> p o j t", j=ROW_TOKENS).to_broadcast([P, 2, ROW_TOKENS, TG])
 
         def multiply_by_tables_on_vector(b, h):
             yT = y_banks[(b, h // 2)]
             nc.vector.scalar_tensor_tensor(
-                out=products[:, b, h, :, :], in0=yT[:, h % 2 : h % 2 + 1, :].to_broadcast([P, 2, P]),
-                scalar=bias[:, h : h + 1], in1=tables[:],
+                out=products[:, b, h // 2, :, :, h % 2, :], in0=twice(yT[:, h % 2 : h % 2 + 1, :]),
+                scalar=bias[:, h : h + 1], in1=tables_by_row,
                 op0=ALU.add, op1=ALU.mult,
             )
 
@@ -159,40 +167,26 @@ def tile_lineartransformerblock_pa_s_kernel(tc, x, cos, sin, Wq_words, Wq_scales
                 out=shifted[:, slot, :], in_=yT[:, h % 2, :], func=ACT.Identity, bias=bias[:, h : h + 1], scale=1.0
             )
             nc.gpsimd.tensor_tensor(
-                out=products[:, b, h, :, :], in0=shifted[:, slot : slot + 1, :].to_broadcast([P, 2, P]),
-                in1=tables[:], op=ALU.mult,
+                out=products[:, b, h // 2, :, :, h % 2, :], in0=twice(shifted[:, slot : slot + 1, :]),
+                in1=tables_by_row, op=ALU.mult,
             )
 
-        def turn_back_and_store(b, pair, by_head):
-            if by_head:
-                for i in range(2):
-                    h = 2 * pair + i
-                    head_ps = psum.tile([P, P], F32, tag="bank%d" % (PAIRS + (2 * pair + i) % PAIRS))
-                    nc.tensor.matmul(
-                        out=head_ps[:], lhsT=products[:, b, h, 0, :], rhs=ident[:],
-                        is_transpose=True, start=True, stop=False,
-                    )
-                    nc.tensor.matmul(
-                        out=head_ps[:], lhsT=products[:, b, h, 1, :], rhs=swap[:],
-                        is_transpose=True, start=False, stop=True,
-                    )
-                    nc.scalar.activation(out=result[:, b, h, :], in_=head_ps[:], func=ACT.Relu)
-                    nc.sync.dma_start(out=out[b, h], in_=result[:, b, h, :])
-            else:
-                rope_ps = psum.tile([P, 2, P], F32, tag="bank%d" % ((PAIRS * (b + 1) + pair) % 8))
-                for i in range(2):
-                    h = 2 * pair + i
-                    nc.tensor.matmul(
-                        out=rope_ps[:, i, :], lhsT=products[:, b, h, 0, :], rhs=ident[:],
-                        is_transpose=True, start=True, stop=False,
-                    )
-                    nc.tensor.matmul(
-                        out=rope_ps[:, i, :], lhsT=products[:, b, h, 1, :], rhs=swap[:],
-                        is_transpose=True, start=False, stop=True,
-                    )
-                heads = slice(2 * pair, 2 * pair + 2)
-                nc.scalar.activation(out=result[:, b, heads, :], in_=rope_ps[:], func=ACT.Relu)
-                nc.sync.dma_start(out=out[b, heads].rearrange("h s d -> s h d"), in_=result[:, b, heads, :])
+        def turn_back_and_store(b, pair):
+            rope_ps = psum.tile([P, ROW_TOKENS, P], F32, tag="bank%d" % ((PAIRS * (b + 1) + pair) % 8))
+            for j in range(ROW_TOKENS):
+                nc.tensor.matmul(
+                    out=rope_ps[:, j, :], lhsT=products[:, b, pair, 0, j, :, :].rearrange("p q t -> p (q t)"),
+                    rhs=ident[:], is_transpose=True, start=True, stop=False,
+                )
+                nc.tensor.matmul(
+                    out=rope_ps[:, j, :], lhsT=products[:, b, pair, 1, j, :, :].rearrange("p q t -> p (q t)"),
+                    rhs=swap[:], is_transpose=True, start=False, stop=True,
+                )
+            nc.scalar.activation(out=result[:, b, pair, :, :], in_=rope_ps[:], func=ACT.Relu)
+            nc.sync.dma_start(
+                out=out[b, 2 * pair : 2 * pair + 2].rearrange("q (t j) d -> (q t) j d", j=ROW_TOKENS),
+                in_=result[:, b, pair, :, :],
+            )
 
         for b, h in SIDE_HEADS:
             multiply_by_tables_on_gpsimd(b, h)
@@ -200,4 +194,4 @@ def tile_lineartransformerblock_pa_s_kernel(tc, x, cos, sin, Wq_words, Wq_scales
             for h in (2 * pair, 2 * pair + 1):
                 if (b, h) not in SIDE_HEADS:
                     multiply_by_tables_on_vector(b, h)
-            turn_back_and_store(b, pair, by_head=(b, pair) in CLOSING_ORDER[-FINE_END:])
+            turn_back_and_store(b, pair)

@@ -148,6 +148,8 @@ def tile_lineartransformerblock_pa_s_kernel(tc, x, cos, sin, Wq_words, Wq_scales
         result = keep.tile([P, B, PAIRS, ROW_TOKENS, P], F32)
         shifted = keep.tile([P, len(SIDE_HEADS), P], F32)
         tables_by_row = tables[:].rearrange("p w (j t) -> p w j t", j=ROW_TOKENS)
+        single = keep.tile([P, 2, 2, P], F32)
+        single_result = keep.tile([P, 2, P], F32)
 
         def twice(values):
             return values.rearrange("p o (j t) -> p o j t", j=ROW_TOKENS).to_broadcast([P, 2, ROW_TOKENS, TG])
@@ -159,6 +161,27 @@ def tile_lineartransformerblock_pa_s_kernel(tc, x, cos, sin, Wq_words, Wq_scales
                 scalar=bias[:, h : h + 1], in1=tables_by_row,
                 op0=ALU.add, op1=ALU.mult,
             )
+
+        def multiply_by_tables_in_token_order(b, h):
+            yT = y_banks[(b, h // 2)]
+            for w in range(2):
+                nc.vector.scalar_tensor_tensor(
+                    out=single[:, h % 2, w, :].rearrange("p (t j) -> p t j", j=ROW_TOKENS),
+                    in0=yT[:, h % 2, :].rearrange("p (j t) -> p t j", j=ROW_TOKENS),
+                    scalar=bias[:, h : h + 1], in1=tables[:, w, :].rearrange("p (j t) -> p t j", j=ROW_TOKENS),
+                    op0=ALU.add, op1=ALU.mult,
+                )
+
+        def turn_head_back_and_store(b, h):
+            head_ps = psum.tile([P, P], F32, tag="bank%d" % (PAIRS + h % PAIRS))
+            nc.tensor.matmul(
+                out=head_ps[:], lhsT=single[:, h % 2, 0, :], rhs=ident[:], is_transpose=True, start=True, stop=False
+            )
+            nc.tensor.matmul(
+                out=head_ps[:], lhsT=single[:, h % 2, 1, :], rhs=swap[:], is_transpose=True, start=False, stop=True
+            )
+            nc.scalar.activation(out=single_result[:, h % 2, :], in_=head_ps[:], func=ACT.Relu)
+            nc.sync.dma_start(out=out[b, h], in_=single_result[:, h % 2, :])
 
         def multiply_by_tables_on_gpsimd(b, h):
             yT = y_banks[(b, h // 2)]
@@ -190,8 +213,12 @@ def tile_lineartransformerblock_pa_s_kernel(tc, x, cos, sin, Wq_words, Wq_scales
 
         for b, h in SIDE_HEADS:
             multiply_by_tables_on_gpsimd(b, h)
-        for b, pair in CLOSING_ORDER:
+        for b, pair in CLOSING_ORDER[:-1]:
             for h in (2 * pair, 2 * pair + 1):
                 if (b, h) not in SIDE_HEADS:
                     multiply_by_tables_on_vector(b, h)
             turn_back_and_store(b, pair)
+        b, pair = CLOSING_ORDER[-1]
+        for h in (2 * pair, 2 * pair + 1):
+            multiply_by_tables_in_token_order(b, h)
+            turn_head_back_and_store(b, h)

@@ -21,11 +21,11 @@ E = 1024
 K_PASS = 512
 G = C // K_PASS
 PAIRS = H // 2
-SIDE_HEADS = [(0, 0), (0, 1), (1, 0)]
-CLOSING_ORDER = [(0, 1), (0, 2), (0, 3), (0, 0), (1, 1), (1, 2), (1, 0), (1, 3)]
+SIDE_HEADS = [(0, 2), (0, 3), (1, 2)]
+CLOSING_ORDER = [(0, 0), (1, 0), (0, 2), (0, 1), (0, 3), (1, 1), (1, 2), (1, 3)]
 WARM_UP = 3
 ROW_TOKENS = 2
-TABLES_AFTER = 2
+TABLES_AFTER = 1
 
 FLOPS = 2 * B * P * C * E
 
@@ -37,11 +37,16 @@ def tile_lineartransformerblock_pa_s_kernel(tc, x, cos, sin, Wq_words, Wq_scales
         psum = ctx.enter_context(tc.psum_pool(name="psum", bufs=1))
         ctx.enter_context(tc.manual_schedule())
 
-        ones = keep.tile([P, 4 * P], BF16)
+        ones = keep.tile([P, 1, P], BF16)
         nc.vector.memset(ones[:], 1.0)
         for i in range(WARM_UP):
-            idle_ps = psum.tile([P, 4 * P], F32, tag="bank5")
-            nc.tensor.matmul(out=idle_ps[:], lhsT=ones[:, 0:P], rhs=ones[:], start=True, stop=True)
+            idle_ps = psum.tile([P, 4, P], F32, tag="bank5")
+            nc.tensor.matmul(
+                out=idle_ps[:], lhsT=ones[:, 0, :], rhs=ones[:].to_broadcast([P, 4, P]), start=True, stop=True
+            )
+
+        sin_sb = keep.tile([P, P], BF16)
+        nc.sync.dma_start(out=sin_sb[:], in_=sin)
 
         x_sb = keep.tile([P, B, C], BF16)
         for b in range(B):
@@ -53,21 +58,25 @@ def tile_lineartransformerblock_pa_s_kernel(tc, x, cos, sin, Wq_words, Wq_scales
         for r in range(4):
             nc.sync.dma_start(out=w_scales[r:P:32, :, :].bitcast(I32), in_=scale_rows[r].bitcast(I32))
 
-        w_bytes = keep.tile([P, G, 2 * E], U8, align_bytes=64)
+        w_halves = [
+            keep.tile([P, G, E], U8, align_bytes=64, name="w_first_heads"),
+            keep.tile([P, G, E], U8, align_bytes=64, name="w_last_heads"),
+        ]
         words_by_partition = Wq_words.rearrange("g p n -> p g n")
-        for half in range(2):
+
+        def load_words(half):
             cols = slice(half * E, (half + 1) * E)
             nc.sync.dma_start(
-                out=w_bytes[:, :, cols].bitcast(I32), in_=words_by_partition[:, :, cols].bitcast(I32)
+                out=w_halves[half][:].bitcast(I32), in_=words_by_partition[:, :, cols].bitcast(I32)
             )
 
-        sin_sb = keep.tile([P, P], BF16)
-        nc.sync.dma_start(out=sin_sb[:], in_=sin)
+        load_words(0)
         cos_sb = keep.tile([P, P], BF16)
         nc.sync.dma_start(out=cos_sb[:], in_=cos)
         bias_rows = keep.tile([P, P], BF16)
         nc.vector.memset(bias_rows[:], 0.0)
         nc.sync.dma_start(out=bias_rows[0:H, :], in_=bq.rearrange("(h d) -> h d", d=P))
+        load_words(1)
 
         ident = keep.tile([P, P], F32)
         make_identity(nc, ident[:])
@@ -79,11 +88,26 @@ def tile_lineartransformerblock_pa_s_kernel(tc, x, cos, sin, Wq_words, Wq_scales
         nc.vector.tensor_copy(out=swap_pairs[:, :, 0], in_=ident_pairs[:, :, 1])
         nc.vector.tensor_copy(out=swap_pairs[:, :, 1], in_=ident_pairs[:, :, 0])
 
+        partner = keep.tile([P, P], BF16)
+        sin_pairs = sin_sb[:].rearrange("p (i two) -> p i two", two=2)
+        partner_pairs = partner[:].rearrange("p (i two) -> p i two", two=2)
+        nc.vector.tensor_copy(out=partner_pairs[:, :, 0], in_=sin_pairs[:, :, 1])
+        nc.vector.tensor_scalar_mul(out=partner_pairs[:, :, 1], in0=sin_pairs[:, :, 0], scalar1=-1.0)
+
+        tables = keep.tile([P, 2, P], BF16)
+        partner_ps = psum.tile([P, P], BF16, tag="bank7")
+
         x_words = x_sb[:].bitcast(F32)
         grouped = keep.tile([P, B, G * P * 4], BF16, align_bytes=64)
         x_codes = keep.tile([P, B, G, P], U32, align_bytes=64)
         x_scales = keep.tile([P, B, G, P], U8, align_bytes=64)
         for b in range(B):
+            if b == 1:
+                nc.tensor.transpose(partner_ps[:], partner[:], ident_bf[:])
+                nc.vector.tensor_copy(
+                    out=tables[:, 1, :].rearrange("p (j t) -> p j t", j=ROW_TOKENS),
+                    in_=partner_ps[:].rearrange("p (t j) -> p j t", j=ROW_TOKENS),
+                )
             for g in range(G):
                 xt = psum.tile([P, 2, P], F32, tag="bank%d" % (G * b + g))
                 for u in range(2):
@@ -109,7 +133,7 @@ def tile_lineartransformerblock_pa_s_kernel(tc, x, cos, sin, Wq_words, Wq_scales
                 for g in range(G):
                     nc.tensor.matmul_mx(
                         out=yT[:, i, :],
-                        lhsT=w_bytes[:, g, 2 * P * h : 2 * P * (h + 1)].bitcast(FP4X4),
+                        lhsT=w_halves[pair // 2][:, g, 2 * P * (h % 4) : 2 * P * (h % 4 + 1)].bitcast(FP4X4),
                         lhsT_scale=w_scales[:, g, P * h : P * (h + 1)],
                         rhs=x_codes[:, b, g, :].bitcast(FP8X4),
                         rhs_scale=x_scales[:, b, g, :],
@@ -120,28 +144,18 @@ def tile_lineartransformerblock_pa_s_kernel(tc, x, cos, sin, Wq_words, Wq_scales
         for pair in range(TABLES_AFTER):
             multiply(0, pair)
 
-        partner = keep.tile([P, P], BF16)
-        sin_pairs = sin_sb[:].rearrange("p (i two) -> p i two", two=2)
-        partner_pairs = partner[:].rearrange("p (i two) -> p i two", two=2)
-        nc.vector.tensor_copy(out=partner_pairs[:, :, 0], in_=sin_pairs[:, :, 1])
-        nc.vector.tensor_scalar_mul(out=partner_pairs[:, :, 1], in0=sin_pairs[:, :, 0], scalar1=-1.0)
-
-        tables_ps = psum.tile([P, 3, P], BF16, tag="bank3")
-        nc.tensor.transpose(tables_ps[:, 0, :], cos_sb[:], ident_bf[:])
-        nc.tensor.transpose(tables_ps[:, 1, :], partner[:], ident_bf[:])
-        nc.tensor.transpose(tables_ps[:, 2, :], bias_rows[:], ident_bf[:])
-        tables = keep.tile([P, 2, P], BF16)
-        nc.vector.tensor_copy(
-            out=tables[:].rearrange("p w (j t) -> p w j t", j=ROW_TOKENS),
-            in_=tables_ps[:, 0:2, :].rearrange("p w (t j) -> p w j t", j=ROW_TOKENS),
+        cos_ps = psum.tile([P, 2, P], BF16, tag="bank3")
+        nc.tensor.transpose(cos_ps[:, 0, :], cos_sb[:], ident_bf[:])
+        nc.tensor.transpose(cos_ps[:, 1, :], bias_rows[:], ident_bf[:])
+        nc.scalar.copy(
+            out=tables[:, 0, :].rearrange("p (j t) -> p j t", j=ROW_TOKENS),
+            in_=cos_ps[:, 0, :].rearrange("p (t j) -> p j t", j=ROW_TOKENS),
         )
         bias = keep.tile([P, H], F32)
-        nc.vector.tensor_copy(out=bias[:], in_=tables_ps[:, 2, 0:H])
+        nc.scalar.copy(out=bias[:], in_=cos_ps[:, 1, 0:H])
 
-        for pair in range(TABLES_AFTER, PAIRS):
-            multiply(0, pair)
-        for pair in range(PAIRS):
-            multiply(1, pair)
+        for b, pair in [(0, 1), (1, 0), (1, 1), (0, 2), (0, 3), (1, 2), (1, 3)]:
+            multiply(b, pair)
 
         TG = P // ROW_TOKENS
         products = keep.tile([P, B, PAIRS, 2, ROW_TOKENS, 2, TG], F32)

@@ -23,7 +23,7 @@ G = C // K_PASS
 PAIRS = H // 2
 SIDE_HEADS = [(0, 2), (0, 3), (1, 2)]
 CLOSING_ORDER = [(0, 0), (1, 0), (0, 2), (0, 1), (0, 3), (1, 1), (1, 2), (1, 3)]
-WARM_UP = 3
+WARM_UP = 5
 ROW_TOKENS = 2
 TABLES_AFTER = 1
 
@@ -37,13 +37,15 @@ def tile_lineartransformerblock_pa_s_kernel(tc, x, cos, sin, Wq_words, Wq_scales
         psum = ctx.enter_context(tc.psum_pool(name="psum", bufs=1))
         ctx.enter_context(tc.manual_schedule())
 
-        ones = keep.tile([P, 1, P], BF16)
+        ones = keep.tile([P, P], F32)
         nc.vector.memset(ones[:], 1.0)
+
+        def idle_product(bank):
+            idle_ps = psum.tile([P, P], F32, tag="bank%d" % bank, name="idle_ps")
+            nc.tensor.matmul(out=idle_ps[:], lhsT=ones[:], rhs=ones[:], start=True, stop=True)
+
         for i in range(WARM_UP):
-            idle_ps = psum.tile([P, 4, P], F32, tag="bank5")
-            nc.tensor.matmul(
-                out=idle_ps[:], lhsT=ones[:, 0, :], rhs=ones[:].to_broadcast([P, 4, P]), start=True, stop=True
-            )
+            idle_product(4 + i % 3)
 
         sin_sb = keep.tile([P, P], BF16)
         nc.sync.dma_start(out=sin_sb[:], in_=sin)
@@ -122,6 +124,8 @@ def tile_lineartransformerblock_pa_s_kernel(tc, x, cos, sin, Wq_words, Wq_scales
                     scales=x_scales[:, b, g, :],
                     in_=grouped[:, b, 512 * g : 512 * (g + 1)],
                 )
+
+        idle_product(6)
 
         y_banks = {}
 

@@ -23,11 +23,17 @@ G = C // K_PASS
 PAIRS = H // 2
 SIDE_HEADS = [(0, 2), (0, 3), (1, 2)]
 CLOSING_ORDER = [(0, 0), (1, 0), (0, 2), (0, 1), (0, 3), (1, 1), (1, 2), (1, 3)]
-WARM_UP = 5
+WARM_UP = 4
+IDLE_COLUMNS = 64
 ROW_TOKENS = 2
-TABLES_AFTER = 1
+FIRST_BANKS = [4, 5]
+Y_BANKS = {(0, 1): 7, (1, 0): 0, (1, 1): 1, (0, 2): 6, (1, 2): 2, (0, 3): 4, (1, 3): 3}
 
 FLOPS = 2 * B * P * C * E
+
+
+def bank_of(b, pair):
+    return Y_BANKS.get((b, pair), FIRST_BANKS[1])
 
 
 def tile_lineartransformerblock_pa_s_kernel(tc, x, cos, sin, Wq_words, Wq_scales, bq, out):
@@ -37,15 +43,18 @@ def tile_lineartransformerblock_pa_s_kernel(tc, x, cos, sin, Wq_words, Wq_scales
         psum = ctx.enter_context(tc.psum_pool(name="psum", bufs=1))
         ctx.enter_context(tc.manual_schedule())
 
-        ones = keep.tile([P, P], F32)
+        ones = keep.tile([P, 1], F32)
         nc.vector.memset(ones[:], 1.0)
 
-        def idle_product(bank):
-            idle_ps = psum.tile([P, P], F32, tag="bank%d" % bank, name="idle_ps")
-            nc.tensor.matmul(out=idle_ps[:], lhsT=ones[:], rhs=ones[:], start=True, stop=True)
+        def idle_product(bank, columns):
+            idle_ps = psum.tile([P, columns], F32, tag="bank%d" % bank, name="idle_ps")
+            nc.tensor.matmul(
+                out=idle_ps[:], lhsT=ones[:].to_broadcast([P, P]), rhs=ones[:].to_broadcast([P, columns]),
+                start=True, stop=True,
+            )
 
         for i in range(WARM_UP):
-            idle_product(4 + i % 3)
+            idle_product(4 + i % 3, P)
 
         sin_sb = keep.tile([P, P], BF16)
         nc.sync.dma_start(out=sin_sb[:], in_=sin)
@@ -125,30 +134,36 @@ def tile_lineartransformerblock_pa_s_kernel(tc, x, cos, sin, Wq_words, Wq_scales
                     in_=grouped[:, b, 512 * g : 512 * (g + 1)],
                 )
 
-        idle_product(6)
+        idle_product(0, IDLE_COLUMNS)
 
         y_banks = {}
 
+        def one_pass(yT, b, h, g):
+            nc.tensor.matmul_mx(
+                out=yT,
+                lhsT=w_halves[h // 4][:, g, 2 * P * (h % 4) : 2 * P * (h % 4 + 1)].bitcast(FP4X4),
+                lhsT_scale=w_scales[:, g, P * h : P * (h + 1)],
+                rhs=x_codes[:, b, g, :].bitcast(FP8X4),
+                rhs_scale=x_scales[:, b, g, :],
+                start=(g == 0),
+                stop=(g == G - 1),
+            )
+
         def multiply(b, pair):
-            yT = psum.tile([P, 2, P], F32, tag="bank%d" % ((PAIRS * (b + 1) + pair) % 8))
-            y_banks[(b, pair)] = yT
+            yT = psum.tile([P, 2, P], F32, tag="bank%d" % Y_BANKS[(b, pair)])
             for i in range(2):
-                h = 2 * pair + i
+                y_banks[(b, 2 * pair + i)] = yT[:, i : i + 1, :]
                 for g in range(G):
-                    nc.tensor.matmul_mx(
-                        out=yT[:, i, :],
-                        lhsT=w_halves[pair // 2][:, g, 2 * P * (h % 4) : 2 * P * (h % 4 + 1)].bitcast(FP4X4),
-                        lhsT_scale=w_scales[:, g, P * h : P * (h + 1)],
-                        rhs=x_codes[:, b, g, :].bitcast(FP8X4),
-                        rhs_scale=x_scales[:, b, g, :],
-                        start=(g == 0),
-                        stop=(g == G - 1),
-                    )
+                    one_pass(yT[:, i, :], b, 2 * pair + i, g)
 
-        for pair in range(TABLES_AFTER):
-            multiply(0, pair)
+        for h in range(2):
+            first_yT = psum.tile([P, 1, P], F32, tag="bank%d" % FIRST_BANKS[h], name="first_yT")
+            y_banks[(0, h)] = first_yT[:, :, :]
+        for g in range(G):
+            for h in range(2):
+                one_pass(y_banks[(0, h)][:, 0, :], 0, h, g)
 
-        cos_ps = psum.tile([P, 2, P], BF16, tag="bank3")
+        cos_ps = psum.tile([P, 2, P], BF16, tag="bank6")
         nc.tensor.transpose(cos_ps[:, 0, :], cos_sb[:], ident_bf[:])
         nc.tensor.transpose(cos_ps[:, 1, :], bias_rows[:], ident_bf[:])
         nc.scalar.copy(
@@ -158,7 +173,7 @@ def tile_lineartransformerblock_pa_s_kernel(tc, x, cos, sin, Wq_words, Wq_scales
         bias = keep.tile([P, H], F32)
         nc.scalar.copy(out=bias[:], in_=cos_ps[:, 1, 0:H])
 
-        for b, pair in [(0, 1), (1, 0), (1, 1), (0, 2), (0, 3), (1, 2), (1, 3)]:
+        for b, pair in Y_BANKS:
             multiply(b, pair)
 
         TG = P // ROW_TOKENS
@@ -173,19 +188,17 @@ def tile_lineartransformerblock_pa_s_kernel(tc, x, cos, sin, Wq_words, Wq_scales
             return values.rearrange("p o (j t) -> p o j t", j=ROW_TOKENS).to_broadcast([P, 2, ROW_TOKENS, TG])
 
         def multiply_by_tables_on_vector(b, h):
-            yT = y_banks[(b, h // 2)]
             nc.vector.scalar_tensor_tensor(
-                out=products[:, b, h // 2, :, :, h % 2, :], in0=twice(yT[:, h % 2 : h % 2 + 1, :]),
+                out=products[:, b, h // 2, :, :, h % 2, :], in0=twice(y_banks[(b, h)]),
                 scalar=bias[:, h : h + 1], in1=tables_by_row,
                 op0=ALU.add, op1=ALU.mult,
             )
 
         def multiply_by_tables_in_token_order(b, h):
-            yT = y_banks[(b, h // 2)]
             for w in range(2):
                 nc.vector.scalar_tensor_tensor(
                     out=single[:, h % 2, w, :].rearrange("p (t j) -> p t j", j=ROW_TOKENS),
-                    in0=yT[:, h % 2, :].rearrange("p (j t) -> p t j", j=ROW_TOKENS),
+                    in0=y_banks[(b, h)].rearrange("p o (j t) -> p (o t) j", j=ROW_TOKENS),
                     scalar=bias[:, h : h + 1], in1=tables[:, w, :].rearrange("p (j t) -> p t j", j=ROW_TOKENS),
                     op0=ALU.add, op1=ALU.mult,
                 )
@@ -202,10 +215,9 @@ def tile_lineartransformerblock_pa_s_kernel(tc, x, cos, sin, Wq_words, Wq_scales
             nc.sync.dma_start(out=out[b, h], in_=single_result[:, h % 2, :])
 
         def multiply_by_tables_on_gpsimd(b, h):
-            yT = y_banks[(b, h // 2)]
             slot = SIDE_HEADS.index((b, h))
             nc.scalar.activation(
-                out=shifted[:, slot, :], in_=yT[:, h % 2, :], func=ACT.Identity, bias=bias[:, h : h + 1], scale=1.0
+                out=shifted[:, slot : slot + 1, :], in_=y_banks[(b, h)], func=ACT.Identity, bias=bias[:, h : h + 1], scale=1.0
             )
             nc.gpsimd.tensor_tensor(
                 out=products[:, b, h // 2, :, :, h % 2, :], in0=twice(shifted[:, slot : slot + 1, :]),
@@ -213,7 +225,7 @@ def tile_lineartransformerblock_pa_s_kernel(tc, x, cos, sin, Wq_words, Wq_scales
             )
 
         def turn_back_and_store(b, pair):
-            rope_ps = psum.tile([P, ROW_TOKENS, P], F32, tag="bank%d" % ((PAIRS * (b + 1) + pair) % 8))
+            rope_ps = psum.tile([P, ROW_TOKENS, P], F32, tag="bank%d" % bank_of(b, pair))
             for j in range(ROW_TOKENS):
                 nc.tensor.matmul(
                     out=rope_ps[:, j, :], lhsT=products[:, b, pair, 0, j, :, :].rearrange("p q t -> p (q t)"),

@@ -56,12 +56,11 @@ def tile_lineartransformerblock_pa_s_kernel(tc, x, cos, sin, Wq_words, Wq_scales
         for i in range(WARM_UP):
             idle_product(4 + i % 3, P)
 
-        sin_sb = keep.tile([P, P], BF16)
-        nc.sync.dma_start(out=sin_sb[:], in_=sin)
-
         x_sb = keep.tile([P, B, C], BF16)
-        for b in range(B):
-            nc.sync.dma_start(out=x_sb[:, b, :], in_=x[b])
+        sin_sb = keep.tile([P, P], BF16)
+        nc.sync.dma_start(out=x_sb[:, 0, :], in_=x[0])
+        nc.sync.dma_start(out=sin_sb[:], in_=sin)
+        nc.sync.dma_start(out=x_sb[:, 1, :], in_=x[1])
 
         w_scales = keep.tile([P, G, E], U8, align_bytes=64)
         nc.vector.memset(w_scales[:].rearrange("p g n -> p (g n)").bitcast(I32), 0)
@@ -163,15 +162,16 @@ def tile_lineartransformerblock_pa_s_kernel(tc, x, cos, sin, Wq_words, Wq_scales
             for h in range(2):
                 one_pass(y_banks[(0, h)][:, 0, :], 0, h, g)
 
-        cos_ps = psum.tile([P, 2, P], BF16, tag="bank6")
-        nc.tensor.transpose(cos_ps[:, 0, :], cos_sb[:], ident_bf[:])
-        nc.tensor.transpose(cos_ps[:, 1, :], bias_rows[:], ident_bf[:])
+        cos_ps = psum.tile([P, P], BF16, tag="bank6")
+        bias_ps = psum.tile([P, P], BF16, tag="bank1")
+        nc.tensor.transpose(cos_ps[:], cos_sb[:], ident_bf[:])
+        nc.tensor.transpose(bias_ps[:], bias_rows[:], ident_bf[:])
         nc.scalar.copy(
             out=tables[:, 0, :].rearrange("p (j t) -> p j t", j=ROW_TOKENS),
-            in_=cos_ps[:, 0, :].rearrange("p (t j) -> p j t", j=ROW_TOKENS),
+            in_=cos_ps[:].rearrange("p (t j) -> p j t", j=ROW_TOKENS),
         )
         bias = keep.tile([P, H], F32)
-        nc.scalar.copy(out=bias[:], in_=cos_ps[:, 1, 0:H])
+        nc.vector.tensor_copy(out=bias[:], in_=bias_ps[:, 0:H])
 
         for b, pair in Y_BANKS:
             multiply(b, pair)

@@ -22,7 +22,7 @@ K_PASS = 512
 G = C // K_PASS
 PAIRS = H // 2
 SIDE_HEADS = [(0, 2), (0, 3), (1, 2)]
-CLOSING_ORDER = [(0, 0), (1, 0), (0, 2), (0, 1), (0, 3), (1, 1), (1, 2), (1, 3)]
+CLOSING_ORDER = [(0, 0), (1, 0), (0, 2), (0, 3), (0, 1), (1, 2), (1, 1), (1, 3)]
 WARM_UP = 4
 IDLE_COLUMNS = 64
 ROW_TOKENS = 2
@@ -62,15 +62,15 @@ def tile_lineartransformerblock_pa_s_kernel(tc, x, cos, sin, Wq_words, Wq_scales
         nc.sync.dma_start(out=sin_sb[:], in_=sin)
         nc.sync.dma_start(out=x_sb[:, 1, :], in_=x[1])
 
-        w_scales = keep.tile([P, G, E], U8, align_bytes=64)
+        w_scales = keep.tile([P, G, E], U8, align_bytes=256)
         nc.vector.memset(w_scales[:].rearrange("p g n -> p (g n)").bitcast(I32), 0)
         scale_rows = Wq_scales.rearrange("g (q r) n -> r q g n", r=4)
         for r in range(4):
             nc.sync.dma_start(out=w_scales[r:P:32, :, :].bitcast(I32), in_=scale_rows[r].bitcast(I32))
 
         w_halves = [
-            keep.tile([P, G, E], U8, align_bytes=64, name="w_first_heads"),
-            keep.tile([P, G, E], U8, align_bytes=64, name="w_last_heads"),
+            keep.tile([P, G, E], U8, align_bytes=256, name="w_first_heads"),
+            keep.tile([P, G, E], U8, align_bytes=256, name="w_last_heads"),
         ]
         words_by_partition = Wq_words.rearrange("g p n -> p g n")
 
@@ -108,9 +108,9 @@ def tile_lineartransformerblock_pa_s_kernel(tc, x, cos, sin, Wq_words, Wq_scales
         partner_ps = psum.tile([P, P], BF16, tag="bank7")
 
         x_words = x_sb[:].bitcast(F32)
-        grouped = keep.tile([P, B, G * P * 4], BF16, align_bytes=64)
-        x_codes = keep.tile([P, B, G, P], U32, align_bytes=64)
-        x_scales = keep.tile([P, B, G, P], U8, align_bytes=64)
+        grouped = keep.tile([P, B, G * P * 4], BF16, align_bytes=256)
+        x_codes = keep.tile([P, B, G, P], U32, align_bytes=256)
+        x_scales = keep.tile([P, B, G, P], U8, align_bytes=256)
         for b in range(B):
             if b == 1:
                 nc.tensor.transpose(partner_ps[:], partner[:], ident_bf[:])

@@ -21,8 +21,8 @@ E = 1024
 K_PASS = 512
 G = C // K_PASS
 PAIRS = H // 2
-SIDE_HEADS = [(0, 2), (0, 3), (1, 2)]
-CLOSING_ORDER = [(0, 0), (1, 0), (0, 2), (0, 3), (0, 1), (1, 2), (1, 1), (1, 3)]
+SIDE_HEADS = [(0, 2), (0, 3)]
+CLOSING_ORDER = [(0, 0), (1, 0), (0, 2), (0, 3), (0, 1), (1, 1), (1, 2), (1, 3)]
 WARM_UP = 4
 IDLE_COLUMNS = 64
 ROW_TOKENS = 2

from contextlib import ExitStack

import concourse.mybir as mybir
from concourse.masks import make_identity

F32 = mybir.dt.float32
BF16 = mybir.dt.bfloat16
I32 = mybir.dt.int32
U8 = mybir.dt.uint8
U32 = mybir.dt.uint32
FP8X4 = mybir.dt.float8_e4m3fn_x4
FP4X4 = mybir.dt.float4_e2m1fn_x4
ALU = mybir.AluOpType
ACT = mybir.ActivationFunctionType

P = 128
B = 2
H = 8
C = 1024
E = 1024
K_PASS = 512
G = C // K_PASS
PAIRS = H // 2
SIDE_HEADS = [(0, 2), (0, 3)]
CLOSING_ORDER = [(0, 0), (1, 0), (0, 2), (0, 3), (0, 1), (1, 1), (1, 2), (1, 3)]
WARM_UP = 4
IDLE_COLUMNS = 64
ROW_TOKENS = 2
FIRST_BANKS = [4, 5]
Y_BANKS = {(0, 1): 7, (1, 0): 0, (1, 1): 1, (0, 2): 6, (1, 2): 2, (0, 3): 4, (1, 3): 3}

FLOPS = 2 * B * P * C * E


def bank_of(b, pair):
    return Y_BANKS.get((b, pair), FIRST_BANKS[1])


def tile_lineartransformerblock_pa_s_kernel(tc, x, cos, sin, Wq_words, Wq_scales, bq, out):
    nc = tc.nc
    with ExitStack() as ctx:
        keep = ctx.enter_context(tc.tile_pool(name="keep", bufs=1))
        psum = ctx.enter_context(tc.psum_pool(name="psum", bufs=1))
        ctx.enter_context(tc.manual_schedule())

        ones = keep.tile([P, 1], F32)
        nc.vector.memset(ones[:], 1.0)

        def idle_product(bank, columns):
            idle_ps = psum.tile([P, columns], F32, tag="bank%d" % bank, name="idle_ps")
            nc.tensor.matmul(
                out=idle_ps[:], lhsT=ones[:].to_broadcast([P, P]), rhs=ones[:].to_broadcast([P, columns]),
                start=True, stop=True,
            )

        for i in range(WARM_UP):
            idle_product(4 + i % 3, P)

        x_sb = keep.tile([P, B, C], BF16)
        sin_sb = keep.tile([P, P], BF16)
        nc.sync.dma_start(out=x_sb[:, 0, :], in_=x[0])
        nc.sync.dma_start(out=sin_sb[:], in_=sin)
        nc.sync.dma_start(out=x_sb[:, 1, :], in_=x[1])

        w_scales = keep.tile([P, G, E], U8, align_bytes=256)
        nc.vector.memset(w_scales[:].rearrange("p g n -> p (g n)").bitcast(I32), 0)
        scale_rows = Wq_scales.rearrange("g (q r) n -> r q g n", r=4)
        for r in range(4):
            nc.sync.dma_start(out=w_scales[r:P:32, :, :].bitcast(I32), in_=scale_rows[r].bitcast(I32))

        w_halves = [
            keep.tile([P, G, E], U8, align_bytes=256, name="w_first_heads"),
            keep.tile([P, G, E], U8, align_bytes=256, name="w_last_heads"),
        ]
        words_by_partition = Wq_words.rearrange("g p n -> p g n")

        def load_words(half):
            cols = slice(half * E, (half + 1) * E)
            nc.sync.dma_start(
                out=w_halves[half][:].bitcast(I32), in_=words_by_partition[:, :, cols].bitcast(I32)
            )

        load_words(0)
        cos_sb = keep.tile([P, P], BF16)
        nc.sync.dma_start(out=cos_sb[:], in_=cos)
        bias_rows = keep.tile([P, P], BF16)
        nc.vector.memset(bias_rows[:], 0.0)
        nc.sync.dma_start(out=bias_rows[0:H, :], in_=bq.rearrange("(h d) -> h d", d=P))
        load_words(1)

        ident = keep.tile([P, P], F32)
        make_identity(nc, ident[:])
        ident_bf = keep.tile([P, P], BF16)
        nc.scalar.copy(out=ident_bf[:], in_=ident[:])
        swap = keep.tile([P, P], F32)
        ident_pairs = ident[:].rearrange("p (i two) -> p i two", two=2)
        swap_pairs = swap[:].rearrange("p (i two) -> p i two", two=2)
        nc.vector.tensor_copy(out=swap_pairs[:, :, 0], in_=ident_pairs[:, :, 1])
        nc.vector.tensor_copy(out=swap_pairs[:, :, 1], in_=ident_pairs[:, :, 0])

        partner = keep.tile([P, P], BF16)
        sin_pairs = sin_sb[:].rearrange("p (i two) -> p i two", two=2)
        partner_pairs = partner[:].rearrange("p (i two) -> p i two", two=2)
        nc.vector.tensor_copy(out=partner_pairs[:, :, 0], in_=sin_pairs[:, :, 1])
        nc.vector.tensor_scalar_mul(out=partner_pairs[:, :, 1], in0=sin_pairs[:, :, 0], scalar1=-1.0)

        tables = keep.tile([P, 2, P], BF16)
        partner_ps = psum.tile([P, P], BF16, tag="bank7")

        x_words = x_sb[:].bitcast(F32)
        grouped = keep.tile([P, B, G * P * 4], BF16, align_bytes=256)
        x_codes = keep.tile([P, B, G, P], U32, align_bytes=256)
        x_scales = keep.tile([P, B, G, P], U8, align_bytes=256)
        for b in range(B):
            if b == 1:
                nc.tensor.transpose(partner_ps[:], partner[:], ident_bf[:])
                nc.vector.tensor_copy(
                    out=tables[:, 1, :].rearrange("p (j t) -> p j t", j=ROW_TOKENS),
                    in_=partner_ps[:].rearrange("p (t j) -> p j t", j=ROW_TOKENS),
                )
            for g in range(G):
                xt = psum.tile([P, 2, P], F32, tag="bank%d" % (G * b + g))
                for u in range(2):
                    nc.tensor.transpose(
                        xt[:, u, :], x_words[:, b, 256 * g + u : 256 * (g + 1) : 2], ident[:]
                    )
                words_out = grouped[:, b, 512 * g : 512 * (g + 1)].bitcast(F32)
                words_out = words_out.rearrange("p (j t u) -> p j t u", j=ROW_TOKENS, u=2)
                nc.scalar.copy(out=words_out, in_=xt[:].rearrange("p u (t j) -> p j t u", j=ROW_TOKENS))
                nc.vector.quantize_mx(
                    out=x_codes[:, b, g, :].bitcast(FP8X4),
                    scales=x_scales[:, b, g, :],
                    in_=grouped[:, b, 512 * g : 512 * (g + 1)],
                )

        idle_product(0, IDLE_COLUMNS)

        y_banks = {}

        def one_pass(yT, b, h, g):
            nc.tensor.matmul_mx(
                out=yT,
                lhsT=w_halves[h // 4][:, g, 2 * P * (h % 4) : 2 * P * (h % 4 + 1)].bitcast(FP4X4),
                lhsT_scale=w_scales[:, g, P * h : P * (h + 1)],
                rhs=x_codes[:, b, g, :].bitcast(FP8X4),
                rhs_scale=x_scales[:, b, g, :],
                start=(g == 0),
                stop=(g == G - 1),
            )

        def multiply(b, pair):
            yT = psum.tile([P, 2, P], F32, tag="bank%d" % Y_BANKS[(b, pair)])
            for i in range(2):
                y_banks[(b, 2 * pair + i)] = yT[:, i : i + 1, :]
                for g in range(G):
                    one_pass(yT[:, i, :], b, 2 * pair + i, g)

        for h in range(2):
            first_yT = psum.tile([P, 1, P], F32, tag="bank%d" % FIRST_BANKS[h], name="first_yT")
            y_banks[(0, h)] = first_yT[:, :, :]
        for g in range(G):
            for h in range(2):
                one_pass(y_banks[(0, h)][:, 0, :], 0, h, g)

        cos_ps = psum.tile([P, P], BF16, tag="bank6")
        bias_ps = psum.tile([P, P], BF16, tag="bank1")
        nc.tensor.transpose(cos_ps[:], cos_sb[:], ident_bf[:])
        nc.tensor.transpose(bias_ps[:], bias_rows[:], ident_bf[:])
        nc.scalar.copy(
            out=tables[:, 0, :].rearrange("p (j t) -> p j t", j=ROW_TOKENS),
            in_=cos_ps[:].rearrange("p (t j) -> p j t", j=ROW_TOKENS),
        )
        bias = keep.tile([P, H], F32)
        nc.vector.tensor_copy(out=bias[:], in_=bias_ps[:, 0:H])

        for b, pair in Y_BANKS:
            multiply(b, pair)

        TG = P // ROW_TOKENS
        products = keep.tile([P, B, PAIRS, 2, ROW_TOKENS, 2, TG], F32)
        result = keep.tile([P, B, PAIRS, ROW_TOKENS, P], F32)
        shifted = keep.tile([P, len(SIDE_HEADS), P], F32)
        tables_by_row = tables[:].rearrange("p w (j t) -> p w j t", j=ROW_TOKENS)
        single = keep.tile([P, 2, 2, P], F32)
        single_result = keep.tile([P, 2, P], F32)

        def twice(values):
            return values.rearrange("p o (j t) -> p o j t", j=ROW_TOKENS).to_broadcast([P, 2, ROW_TOKENS, TG])

        def multiply_by_tables_on_vector(b, h):
            nc.vector.scalar_tensor_tensor(
                out=products[:, b, h // 2, :, :, h % 2, :], in0=twice(y_banks[(b, h)]),
                scalar=bias[:, h : h + 1], in1=tables_by_row,
                op0=ALU.add, op1=ALU.mult,
            )

        def multiply_by_tables_in_token_order(b, h):
            for w in range(2):
                nc.vector.scalar_tensor_tensor(
                    out=single[:, h % 2, w, :].rearrange("p (t j) -> p t j", j=ROW_TOKENS),
                    in0=y_banks[(b, h)].rearrange("p o (j t) -> p (o t) j", j=ROW_TOKENS),
                    scalar=bias[:, h : h + 1], in1=tables[:, w, :].rearrange("p (j t) -> p t j", j=ROW_TOKENS),
                    op0=ALU.add, op1=ALU.mult,
                )

        def turn_head_back_and_store(b, h):
            head_ps = psum.tile([P, P], F32, tag="bank%d" % (PAIRS + h % PAIRS))
            nc.tensor.matmul(
                out=head_ps[:], lhsT=single[:, h % 2, 0, :], rhs=ident[:], is_transpose=True, start=True, stop=False
            )
            nc.tensor.matmul(
                out=head_ps[:], lhsT=single[:, h % 2, 1, :], rhs=swap[:], is_transpose=True, start=False, stop=True
            )
            nc.scalar.activation(out=single_result[:, h % 2, :], in_=head_ps[:], func=ACT.Relu)
            nc.sync.dma_start(out=out[b, h], in_=single_result[:, h % 2, :])

        def multiply_by_tables_on_gpsimd(b, h):
            slot = SIDE_HEADS.index((b, h))
            nc.scalar.activation(
                out=shifted[:, slot : slot + 1, :], in_=y_banks[(b, h)], func=ACT.Identity, bias=bias[:, h : h + 1], scale=1.0
            )
            nc.gpsimd.tensor_tensor(
                out=products[:, b, h // 2, :, :, h % 2, :], in0=twice(shifted[:, slot : slot + 1, :]),
                in1=tables_by_row, op=ALU.mult,
            )

        def turn_back_and_store(b, pair):
            rope_ps = psum.tile([P, ROW_TOKENS, P], F32, tag="bank%d" % bank_of(b, pair))
            for j in range(ROW_TOKENS):
                nc.tensor.matmul(
                    out=rope_ps[:, j, :], lhsT=products[:, b, pair, 0, j, :, :].rearrange("p q t -> p (q t)"),
                    rhs=ident[:], is_transpose=True, start=True, stop=False,
                )
                nc.tensor.matmul(
                    out=rope_ps[:, j, :], lhsT=products[:, b, pair, 1, j, :, :].rearrange("p q t -> p (q t)"),
                    rhs=swap[:], is_transpose=True, start=False, stop=True,
                )
            nc.scalar.activation(out=result[:, b, pair, :, :], in_=rope_ps[:], func=ACT.Relu)
            nc.sync.dma_start(
                out=out[b, 2 * pair : 2 * pair + 2].rearrange("q (t j) d -> (q t) j d", j=ROW_TOKENS),
                in_=result[:, b, pair, :, :],
            )

        for b, h in SIDE_HEADS:
            multiply_by_tables_on_gpsimd(b, h)
        for b, pair in CLOSING_ORDER[:-1]:
            for h in (2 * pair, 2 * pair + 1):
                if (b, h) not in SIDE_HEADS:
                    multiply_by_tables_on_vector(b, h)
            turn_back_and_store(b, pair)
        b, pair = CLOSING_ORDER[-1]
        for h in (2 * pair, 2 * pair + 1):
            multiply_by_tables_in_token_order(b, h)
            turn_head_back_and_store(b, h)
